import numpy as np
import ml_dtypes


def mxq(x, axis, fmt="e4m3"):
    dtype, down = {"e4m3": (ml_dtypes.float8_e4m3fn, 7), "e5m2": (ml_dtypes.float8_e5m2, 14)}[fmt]
    v = np.moveaxis(np.asarray(x, np.float32).astype(ml_dtypes.bfloat16).astype(np.float64), axis, -1)
    blocks = v.reshape(v.shape[:-1] + (-1, 32))
    amax = np.abs(blocks).max(-1, keepdims=True)
    byte = np.maximum(np.where(amax > 0, np.frexp(amax)[1] - 1 + 127, 0) - down, 1)
    scale = np.exp2(byte - 127.0)
    codes = (blocks / scale).astype(np.float32).astype(dtype).astype(np.float64)
    return np.moveaxis((codes * scale).reshape(v.shape), -1, axis)


WIDE = False


def mx_kscale(k):
    if not WIDE:
        return np.ones(k)
    levels = np.array([10, -10, 5, -5, 0])
    if k % 512:
        return np.exp2(np.random.permutation(np.resize(levels, k // 32))).repeat(32)
    a = np.empty((k // 512, 16))
    for p in range(k // 512):
        a[p, :8] = np.random.permutation(np.resize(levels, 8))
        for g in range(8):
            far = levels[np.abs(levels - a[p, g]) >= 10]
            a[p, g + 8] = far[np.random.randint(len(far))]
    return np.exp2(a.ravel()).repeat(32)


BF16 = ml_dtypes.bfloat16


def bf(x):
    return np.asarray(x, np.float32).astype(BF16)


def f64(x):
    return np.asarray(x).astype(np.float64)


B, T, D, E, F = 4, 256, 1024, 1024, 4096
EPS = 1e-6


def rms_norm(x, w):
    rms = np.sqrt(np.mean(x * x, axis=-1, keepdims=True) + EPS)
    return x / rms * w


def erf(v):
    a = np.minimum(np.abs(v), 6.0)
    z = 2.0 * a * a
    term = a.copy()
    tot = a.copy()
    for n in range(1, 110):
        term = term * z / (2 * n + 1)
        tot = tot + term
    return np.sign(v) * tot * np.exp(-a * a) * 2.0 / np.sqrt(np.pi)


def gelu_erf(v):
    return 0.5 * v * (1.0 + erf(v / np.sqrt(2.0)))


def setup_inputs():
    s, t = mx_kscale(E), mx_kscale(D)
    return {"attn": bf(np.random.standard_normal((B, T, E)) * 0.6 * s),
            "x": bf(np.random.standard_normal((B, T, D))),
            "wo": bf(np.random.standard_normal((E, D)) / np.sqrt(E) / s[:, None]),
            "bo": bf(np.random.standard_normal(D) * 0.1),
            "mlp_norm_w": bf((1.0 + 0.1 * np.random.standard_normal(D)) * t),
            "w1": bf(np.random.standard_normal((D, F)) / np.sqrt(D) / t[:, None]),
            "b1": bf(np.random.standard_normal(F) * 0.1)}


def reference(attn, x, wo, bo, mlp_norm_w, w1, b1):
    x_mid = f64(x) + (mxq(f64(attn), 2, "e4m3") @ mxq(f64(wo), 0, "e4m3")) + f64(bo)
    h = rms_norm(x_mid, f64(mlp_norm_w))
    g = gelu_erf((mxq(h, 2, "e4m3") @ mxq(f64(w1), 0, "e4m3")) + f64(b1))
    return x_mid, g

@@ -1,0 +1,278 @@
+from contextlib import ExitStack
+
+import concourse.mybir as mybir
+from concourse.masks import make_identity
+
+F32 = mybir.dt.float32
+BF16 = mybir.dt.bfloat16
+U32 = mybir.dt.uint32
+U8 = mybir.dt.uint8
+FP8X4 = mybir.dt.float8_e4m3fn_x4
+ALU = mybir.AluOpType
+ACT = mybir.ActivationFunctionType
+
+P = 128
+PACK = 4
+K_PASS = P * PACK
+BANK = 512
+
+TOKENS = 4 * 256
+E = 1024
+D = 1024
+F = 4096
+EPS = 1e-6
+
+TOKEN_TILES = TOKENS // P
+PASSES = D // K_PASS
+UNIT = 1024
+QUARTERS = F // UNIT
+
+WEIGHT_UNITS = PASSES * (D // UNIT) + PASSES * QUARTERS
+LAG = 3
+
+FLOPS = 2 * TOKENS * E * D + 2 * TOKENS * D * F
+
+
+def tile_tinyblock_pb_kernel(tc, attn, x, wo, bo, mlp_norm_w, w1, b1, out_0, out_1):
+    nc = tc.nc
+    attn_rows = attn.flatten_outer_dims()
+    x_rows = x.flatten_outer_dims()
+    x_mid_rows = out_0.flatten_outer_dims()
+    g_rows = out_1.flatten_outer_dims()
+
+    with ExitStack() as stack:
+        keep = stack.enter_context(tc.tile_pool(name="keep", bufs=1))
+        raw_pool = stack.enter_context(tc.tile_pool(name="raw", bufs=5))
+        grouped_pool = stack.enter_context(tc.tile_pool(name="grouped", bufs=3))
+        work = stack.enter_context(tc.tile_pool(name="work", bufs=2))
+        result = stack.enter_context(tc.tile_pool(name="result", bufs=6))
+        psum_t = stack.enter_context(tc.psum_pool(name="psum_t", bufs=1))
+        psum_1 = stack.enter_context(tc.psum_pool(name="psum_1", bufs=2))
+        psum_2 = stack.enter_context(tc.psum_pool(name="psum_2", bufs=4))
+
+        minus_half = keep.tile([P, 1], F32)
+        nc.vector.memset(minus_half[:], -0.5)
+        table_warm = keep.tile([P, 1], F32)
+        nc.scalar.activation(out=table_warm[:], in_=minus_half[:], func=ACT.Gelu)
+        ident_f32 = keep.tile([P, P], F32)
+        make_identity(nc, ident_f32[:])
+
+        wo_codes = keep.tile([P, PASSES, D], U32, align_bytes=64)
+        wo_scales = keep.tile([P, PASSES, D], U8, align_bytes=64)
+        w1_codes = keep.tile([P, PASSES, F], U32, align_bytes=64)
+        w1_scales = keep.tile([P, PASSES, F], U8, align_bytes=64)
+
+        attn_sb = [keep.tile([P, E], BF16, name="attn%d" % j) for j in range(TOKEN_TILES)]
+        x_sb = [keep.tile([P, D], BF16, name="x%d" % j) for j in range(TOKEN_TILES)]
+        bo_all = keep.tile([P, D], BF16)
+        gain_all = keep.tile([P, D], BF16)
+        b1_all = keep.tile([P, F], BF16)
+
+        def load_tokens(j):
+            rows = slice(j * P, (j + 1) * P)
+            nc.sync.dma_start(out=attn_sb[j][:], in_=attn_rows[rows, :])
+            nc.sync.dma_start(out=x_sb[j][:], in_=x_rows[rows, :])
+
+        def load_wo_unit(g):
+            raw = raw_pool.tile([P, PACK, UNIT], BF16, name="wo_raw%d" % g, tag="raw")
+            nc.sync.dma_start(
+                out=raw[:], in_=wo[g * K_PASS : (g + 1) * K_PASS, :].rearrange("(p t) n -> p t n", t=PACK)
+            )
+            return raw
+
+        def load_w1_unit(q, g):
+            raw = raw_pool.tile([P, PACK, UNIT], BF16, name="w1_raw%d_%d" % (q, g), tag="raw")
+            nc.sync.dma_start(
+                out=raw[:],
+                in_=w1[g * K_PASS : (g + 1) * K_PASS, q * UNIT : (q + 1) * UNIT].rearrange(
+                    "(p t) n -> p t n", t=PACK
+                ),
+            )
+            return raw
+
+        units = []
+        nc.sync.dma_start(out=attn_sb[0][:], in_=attn_rows[0:P, :])
+        for g in range(PASSES):
+            units.append((load_wo_unit(g), wo_codes[:, g, :], wo_scales[:, g, :]))
+        nc.sync.dma_start(out=bo_all[:], in_=bo.partition_broadcast(P))
+        nc.sync.dma_start(out=x_sb[0][:], in_=x_rows[0:P, :])
+        for j in range(1, LAG):
+            load_tokens(j)
+        nc.sync.dma_start(out=gain_all[:], in_=mlp_norm_w.partition_broadcast(P))
+        for q in range(QUARTERS):
+            cols = slice(q * UNIT, (q + 1) * UNIT)
+            for g in range(PASSES):
+                units.append((load_w1_unit(q, g), w1_codes[:, g, cols], w1_scales[:, g, cols]))
+            if q == 0:
+                nc.sync.dma_start(out=b1_all[:], in_=b1.partition_broadcast(P))
+        for j in range(LAG, TOKEN_TILES):
+            load_tokens(j)
+
+        grouped_tiles = []
+
+        def weight_step(s):
+            if s < WEIGHT_UNITS:
+                raw = units[s][0]
+                grouped = grouped_pool.tile([P, UNIT, PACK], BF16, align_bytes=64)
+                half = UNIT // 2
+                nc.vector.tensor_copy(
+                    out=grouped[:, 0:half, :].rearrange("p (c i) t -> p c t i", i=4),
+                    in_=raw[:, :, 0:half].rearrange("p t (c i) -> p c t i", i=4),
+                )
+                nc.scalar.copy(
+                    out=grouped[:, half:UNIT, :].rearrange("p (c i) t -> p c t i", i=4),
+                    in_=raw[:, :, half:UNIT].rearrange("p t (c i) -> p c t i", i=4),
+                )
+                grouped_tiles.append(grouped)
+            if s >= 1:
+                nc.vector.quantize_mx(
+                    out=units[s - 1][1].bitcast(FP8X4),
+                    scales=units[s - 1][2],
+                    in_=grouped_tiles[s - 1][:].rearrange("p w t -> p (w t)"),
+                )
+
+        attn_grouped, attn_mx, x_bo, acc_1, x_mid, inv_rms, h, h_grouped, h_mx = ({} for n in range(9))
+
+        def transpose_attn(j):
+            words = attn_sb[j][:].bitcast(F32)
+            attn_t = psum_t.tile([P, PACK, P], F32)
+            for g in range(PASSES):
+                for u in range(2):
+                    nc.tensor.transpose(
+                        attn_t[:, 2 * g + u, :], words[:, 2 * P * g + u : 2 * P * (g + 1) : 2], ident_f32[:]
+                    )
+            grouped = work.tile([P, PASSES * P * PACK], BF16, align_bytes=64, name="attn_grouped")
+            nc.scalar.copy(
+                out=grouped[:].bitcast(F32).rearrange("p (g r u) -> p g r u", g=PASSES, u=2),
+                in_=attn_t[:].rearrange("p (g u) r -> p g r u", u=2),
+            )
+            attn_grouped[j] = grouped
+
+        def quantise_attn(j):
+            codes = work.tile([P, PASSES * P], U32, align_bytes=64, name="attn_codes")
+            scales = work.tile([P, PASSES * P], U8, align_bytes=64, name="attn_scales")
+            nc.vector.quantize_mx(out=codes[:].bitcast(FP8X4), scales=scales[:], in_=attn_grouped[j][:])
+            attn_mx[j] = (codes, scales)
+
+        def add_bo_to_x(j):
+            total = work.tile([P, D], F32, name="x_bo")
+            nc.gpsimd.tensor_tensor(out=total[:], in0=x_sb[j][:], in1=bo_all[:], op=ALU.add)
+            x_bo[j] = total
+
+        def first_matmul(j):
+            codes, scales = attn_mx[j]
+            acc_1[j] = []
+            for n in range(D // BANK):
+                cols = slice(n * BANK, (n + 1) * BANK)
+                acc = psum_1.tile([P, BANK], F32, name="acc_1")
+                for g in range(PASSES):
+                    toks = slice(g * P, (g + 1) * P)
+                    nc.tensor.matmul_mx(
+                        out=acc[:],
+                        lhsT=codes[:, toks].bitcast(FP8X4),
+                        lhsT_scale=scales[:, toks],
+                        rhs=wo_codes[:, g, cols].bitcast(FP8X4),
+                        rhs_scale=wo_scales[:, g, cols],
+                        start=(g == 0),
+                        stop=(g == PASSES - 1),
+                    )
+                acc_1[j].append(acc)
+
+        def residual_and_rms(j):
+            total = work.tile([P, D], F32, name="x_mid", bufs=3)
+            for n in range(D // BANK):
+                cols = slice(n * BANK, (n + 1) * BANK)
+                nc.vector.tensor_tensor(out=total[:, cols], in0=acc_1[j][n][:], in1=x_bo[j][:, cols], op=ALU.add)
+            nc.sync.dma_start(out=x_mid_rows[j * P : (j + 1) * P, :], in_=total[:])
+            squares = work.tile([P, D], BF16)
+            mean_sq = work.tile([P, 1], F32)
+            nc.scalar.activation(out=squares[:], in_=total[:], func=ACT.Square, scale=D**-0.5, accum_out=mean_sq[:])
+            mean_eps = work.tile([P, 1], F32)
+            nc.gpsimd.tensor_scalar(out=mean_eps[:], in0=mean_sq[:], scalar1=EPS, scalar2=None, op0=ALU.add)
+            power = work.tile([P, 1], F32, name="inv_rms")
+            nc.gpsimd.tensor_tensor(out=power[:], in0=mean_eps[:], in1=minus_half[:], op=ALU.pow)
+            x_mid[j] = total
+            inv_rms[j] = power
+
+        def normalise(j):
+            normed = work.tile([P, D], BF16, name="h")
+            nc.vector.scalar_tensor_tensor(
+                out=normed[:], in0=x_mid[j][:], scalar=inv_rms[j][:, 0:1], in1=gain_all[:], op0=ALU.mult, op1=ALU.mult
+            )
+            h[j] = normed
+
+        def transpose_h(j):
+            words = h[j][:].bitcast(F32)
+            h_t = psum_t.tile([P, PACK, P], F32)
+            for g in range(PASSES):
+                for u in range(2):
+                    nc.tensor.transpose(
+                        h_t[:, 2 * g + u, :], words[:, 2 * P * g + u : 2 * P * (g + 1) : 2], ident_f32[:]
+                    )
+            grouped = work.tile([P, PASSES * P * PACK], BF16, align_bytes=64, name="h_grouped")
+            nc.scalar.copy(
+                out=grouped[:].bitcast(F32).rearrange("p (g r u) -> p g r u", g=PASSES, u=2),
+                in_=h_t[:].rearrange("p (g u) r -> p g r u", u=2),
+            )
+            h_grouped[j] = grouped
+
+        def quantise_h(j):
+            codes = work.tile([P, PASSES * P], U32, align_bytes=64, name="h_codes")
+            scales = work.tile([P, PASSES * P], U8, align_bytes=64, name="h_scales")
+            nc.vector.quantize_mx(
+                out=codes[:].bitcast(FP8X4), scales=scales[:], in_=h_grouped[j][:]
+            )
+            h_mx[j] = (codes, scales)
+
+        def second_stage(j, q):
+            codes, scales = h_mx[j]
+            g_tile = result.tile([P, UNIT], F32)
+            for n in range(UNIT // BANK):
+                cols = slice(q * UNIT + n * BANK, q * UNIT + (n + 1) * BANK)
+                acc = psum_2.tile([P, BANK], F32, name="acc_2")
+                for g in range(PASSES):
+                    toks = slice(g * P, (g + 1) * P)
+                    nc.tensor.matmul_mx(
+                        out=acc[:],
+                        lhsT=codes[:, toks].bitcast(FP8X4),
+                        lhsT_scale=scales[:, toks],
+                        rhs=w1_codes[:, g, cols].bitcast(FP8X4),
+                        rhs_scale=w1_scales[:, g, cols],
+                        start=(g == 0),
+                        stop=(g == PASSES - 1),
+                    )
+                nc.vector.tensor_tensor(
+                    out=g_tile[:, n * BANK : (n + 1) * BANK], in0=acc[:], in1=b1_all[:, cols], op=ALU.add
+                )
+            nc.scalar.activation(out=g_tile[:], in_=g_tile[:], func=ACT.Gelu)
+            nc.sync.dma_start(out=g_rows[j * P : (j + 1) * P, q * UNIT : (q + 1) * UNIT], in_=g_tile[:])
+
+        def live(j):
+            return 0 <= j < TOKEN_TILES
+
+        steps_a_round = (WEIGHT_UNITS + 1 + LAG - 1) // LAG
+        for i in range(-LAG, TOKEN_TILES):
+            if live(i + 3):
+                transpose_attn(i + 3)
+            if live(i + 1):
+                transpose_h(i + 1)
+            if live(i + 2):
+                residual_and_rms(i + 2)
+            if live(i + 3):
+                add_bo_to_x(i + 3)
+                quantise_attn(i + 3)
+            if live(i + 1):
+                quantise_h(i + 1)
+            if i < 0:
+                first_step = (i + LAG) * steps_a_round
+                for s in range(first_step, min(first_step + steps_a_round, WEIGHT_UNITS + 1)):
+                    weight_step(s)
+            else:
+                for q in range(QUARTERS - 1):
+                    second_stage(i, q)
+            if live(i + 2):
+                normalise(i + 2)
+            if i >= 0:
+                second_stage(i, QUARTERS - 1)
+            if live(i + 3):
+                first_matmul(i + 3)

@@ -27,7 +27,7 @@ PASSES = D // K_PASS
 UNIT = 1024
 QUARTERS = F // UNIT
 
-WEIGHT_UNITS = PASSES * (D // UNIT) + PASSES * QUARTERS
+WEIGHT_UNITS = PASSES * (D // BANK) + PASSES * QUARTERS
 LAG = 3
 
 FLOPS = 2 * TOKENS * E * D + 2 * TOKENS * D * F
@@ -48,12 +48,19 @@ def tile_tinyblock_pb_kernel(tc, attn, x, wo, bo, mlp_norm_w, w1, b1, out_0, out
         result = stack.enter_context(tc.tile_pool(name="result", bufs=6))
         psum_t = stack.enter_context(tc.psum_pool(name="psum_t", bufs=1))
         psum_1 = stack.enter_context(tc.psum_pool(name="psum_1", bufs=2))
-        psum_2 = stack.enter_context(tc.psum_pool(name="psum_2", bufs=4))
+        psum_2 = stack.enter_context(tc.psum_pool(name="psum_2", bufs=3))
+        psum_x = stack.enter_context(tc.psum_pool(name="psum_x", bufs=1))
 
         minus_half = keep.tile([P, 1], F32)
         nc.vector.memset(minus_half[:], -0.5)
         table_warm = keep.tile([P, 1], F32)
         nc.scalar.activation(out=table_warm[:], in_=minus_half[:], func=ACT.Gelu)
+        ident_bf16 = keep.tile([P, P], BF16)
+        make_identity(nc, ident_bf16[:])
+        ones = keep.tile([P, P], BF16)
+        nc.vector.memset(ones[:], 1.0)
+        bo_row = keep.tile([P, D], BF16)
+        nc.gpsimd.memset(bo_row[:].bitcast(F32), 0.0)
         ident_f32 = keep.tile([P, P], F32)
         make_identity(nc, ident_f32[:])
 
@@ -64,7 +71,6 @@ def tile_tinyblock_pb_kernel(tc, attn, x, wo, bo, mlp_norm_w, w1, b1, out_0, out
 
         attn_sb = [keep.tile([P, E], BF16, name="attn%d" % j) for j in range(TOKEN_TILES)]
         x_sb = [keep.tile([P, D], BF16, name="x%d" % j) for j in range(TOKEN_TILES)]
-        bo_all = keep.tile([P, D], BF16)
         gain_all = keep.tile([P, D], BF16)
         b1_all = keep.tile([P, F], BF16)
 
@@ -73,10 +79,11 @@ def tile_tinyblock_pb_kernel(tc, attn, x, wo, bo, mlp_norm_w, w1, b1, out_0, out
             nc.sync.dma_start(out=attn_sb[j][:], in_=attn_rows[rows, :])
             nc.sync.dma_start(out=x_sb[j][:], in_=x_rows[rows, :])
 
-        def load_wo_unit(g):
-            raw = raw_pool.tile([P, PACK, UNIT], BF16, name="wo_raw%d" % g, tag="raw")
+        def load_wo_unit(g, cols):
+            width = cols.stop - cols.start
+            raw = raw_pool.tile([P, PACK, width], BF16, name="wo_raw%d_%d" % (g, cols.start), tag="raw")
             nc.sync.dma_start(
-                out=raw[:], in_=wo[g * K_PASS : (g + 1) * K_PASS, :].rearrange("(p t) n -> p t n", t=PACK)
+                out=raw[:], in_=wo[g * K_PASS : (g + 1) * K_PASS, cols].rearrange("(p t) n -> p t n", t=PACK)
             )
             return raw
 
@@ -93,17 +100,20 @@ def tile_tinyblock_pb_kernel(tc, attn, x, wo, bo, mlp_norm_w, w1, b1, out_0, out
         units = []
         nc.sync.dma_start(out=attn_sb[0][:], in_=attn_rows[0:P, :])
         for g in range(PASSES):
-            units.append((load_wo_unit(g), wo_codes[:, g, :], wo_scales[:, g, :]))
-        nc.sync.dma_start(out=bo_all[:], in_=bo.partition_broadcast(P))
+            for n in range(D // BANK):
+                cols = slice(n * BANK, (n + 1) * BANK)
+                units.append((load_wo_unit(g, cols), wo_codes[:, g, cols], wo_scales[:, g, cols]))
+        nc.sync.dma_start(out=bo_row[0:1, :], in_=bo.unsqueeze(0))
         nc.sync.dma_start(out=x_sb[0][:], in_=x_rows[0:P, :])
-        for j in range(1, LAG):
-            load_tokens(j)
-        nc.sync.dma_start(out=gain_all[:], in_=mlp_norm_w.partition_broadcast(P))
         for q in range(QUARTERS):
             cols = slice(q * UNIT, (q + 1) * UNIT)
             for g in range(PASSES):
                 units.append((load_w1_unit(q, g), w1_codes[:, g, cols], w1_scales[:, g, cols]))
-            if q == 0:
+                if q == 0:
+                    load_tokens(g + 1)
+                    if g == 0:
+                        nc.sync.dma_start(out=gain_all[:], in_=mlp_norm_w.partition_broadcast(P))
+            if q == 1:
                 nc.sync.dma_start(out=b1_all[:], in_=b1.partition_broadcast(P))
         for j in range(LAG, TOKEN_TILES):
             load_tokens(j)
@@ -113,15 +123,16 @@ def tile_tinyblock_pb_kernel(tc, attn, x, wo, bo, mlp_norm_w, w1, b1, out_0, out
         def weight_step(s):
             if s < WEIGHT_UNITS:
                 raw = units[s][0]
-                grouped = grouped_pool.tile([P, UNIT, PACK], BF16, align_bytes=64)
-                half = UNIT // 2
+                width = raw.shape[2]
+                grouped = grouped_pool.tile([P, width, PACK], BF16, align_bytes=64)
+                half = width // 2
                 nc.vector.tensor_copy(
                     out=grouped[:, 0:half, :].rearrange("p (c i) t -> p c t i", i=4),
                     in_=raw[:, :, 0:half].rearrange("p t (c i) -> p c t i", i=4),
                 )
                 nc.scalar.copy(
-                    out=grouped[:, half:UNIT, :].rearrange("p (c i) t -> p c t i", i=4),
-                    in_=raw[:, :, half:UNIT].rearrange("p t (c i) -> p c t i", i=4),
+                    out=grouped[:, half:width, :].rearrange("p (c i) t -> p c t i", i=4),
+                    in_=raw[:, :, half:width].rearrange("p t (c i) -> p c t i", i=4),
                 )
                 grouped_tiles.append(grouped)
             if s >= 1:
@@ -156,7 +167,12 @@ def tile_tinyblock_pb_kernel(tc, attn, x, wo, bo, mlp_norm_w, w1, b1, out_0, out
 
         def add_bo_to_x(j):
             total = work.tile([P, D], F32, name="x_bo")
-            nc.gpsimd.tensor_tensor(out=total[:], in0=x_sb[j][:], in1=bo_all[:], op=ALU.add)
+            for n in range(D // BANK):
+                cols = slice(n * BANK, (n + 1) * BANK)
+                bank = psum_x.tile([P, BANK], F32)
+                nc.tensor.matmul(out=bank[:], lhsT=ident_bf16[:], rhs=x_sb[j][:, cols], start=True, stop=False)
+                nc.tensor.matmul(out=bank[:], lhsT=ones[:], rhs=bo_row[:, cols], start=False, stop=True)
+                nc.scalar.copy(out=total[:, cols], in_=bank[:])
             x_bo[j] = total
 
         def first_matmul(j):

from contextlib import ExitStack

import concourse.mybir as mybir
from concourse.masks import make_identity

F32 = mybir.dt.float32
BF16 = mybir.dt.bfloat16
U32 = mybir.dt.uint32
U8 = mybir.dt.uint8
FP8X4 = mybir.dt.float8_e4m3fn_x4
ALU = mybir.AluOpType
ACT = mybir.ActivationFunctionType

P = 128
PACK = 4
K_PASS = P * PACK
BANK = 512

TOKENS = 4 * 256
E = 1024
D = 1024
F = 4096
EPS = 1e-6

TOKEN_TILES = TOKENS // P
PASSES = D // K_PASS
UNIT = 1024
QUARTERS = F // UNIT

WEIGHT_UNITS = PASSES * (D // BANK) + PASSES * QUARTERS
LAG = 3

FLOPS = 2 * TOKENS * E * D + 2 * TOKENS * D * F


def tile_tinyblock_pb_kernel(tc, attn, x, wo, bo, mlp_norm_w, w1, b1, out_0, out_1):
    nc = tc.nc
    attn_rows = attn.flatten_outer_dims()
    x_rows = x.flatten_outer_dims()
    x_mid_rows = out_0.flatten_outer_dims()
    g_rows = out_1.flatten_outer_dims()

    with ExitStack() as stack:
        keep = stack.enter_context(tc.tile_pool(name="keep", bufs=1))
        raw_pool = stack.enter_context(tc.tile_pool(name="raw", bufs=5))
        grouped_pool = stack.enter_context(tc.tile_pool(name="grouped", bufs=3))
        work = stack.enter_context(tc.tile_pool(name="work", bufs=2))
        result = stack.enter_context(tc.tile_pool(name="result", bufs=6))
        psum_t = stack.enter_context(tc.psum_pool(name="psum_t", bufs=1))
        psum_1 = stack.enter_context(tc.psum_pool(name="psum_1", bufs=2))
        psum_2 = stack.enter_context(tc.psum_pool(name="psum_2", bufs=3))
        psum_x = stack.enter_context(tc.psum_pool(name="psum_x", bufs=1))

        minus_half = keep.tile([P, 1], F32)
        nc.vector.memset(minus_half[:], -0.5)
        table_warm = keep.tile([P, 1], F32)
        nc.scalar.activation(out=table_warm[:], in_=minus_half[:], func=ACT.Gelu)
        ident_bf16 = keep.tile([P, P], BF16)
        make_identity(nc, ident_bf16[:])
        ones = keep.tile([P, P], BF16)
        nc.vector.memset(ones[:], 1.0)
        bo_row = keep.tile([P, D], BF16)
        nc.gpsimd.memset(bo_row[:].bitcast(F32), 0.0)
        ident_f32 = keep.tile([P, P], F32)
        make_identity(nc, ident_f32[:])

        wo_codes = keep.tile([P, PASSES, D], U32, align_bytes=64)
        wo_scales = keep.tile([P, PASSES, D], U8, align_bytes=64)
        w1_codes = keep.tile([P, PASSES, F], U32, align_bytes=64)
        w1_scales = keep.tile([P, PASSES, F], U8, align_bytes=64)

        attn_sb = [keep.tile([P, E], BF16, name="attn%d" % j) for j in range(TOKEN_TILES)]
        x_sb = [keep.tile([P, D], BF16, name="x%d" % j) for j in range(TOKEN_TILES)]
        gain_all = keep.tile([P, D], BF16)
        b1_all = keep.tile([P, F], BF16)

        def load_tokens(j):
            rows = slice(j * P, (j + 1) * P)
            nc.sync.dma_start(out=attn_sb[j][:], in_=attn_rows[rows, :])
            nc.sync.dma_start(out=x_sb[j][:], in_=x_rows[rows, :])

        def load_wo_unit(g, cols):
            width = cols.stop - cols.start
            raw = raw_pool.tile([P, PACK, width], BF16, name="wo_raw%d_%d" % (g, cols.start), tag="raw")
            nc.sync.dma_start(
                out=raw[:], in_=wo[g * K_PASS : (g + 1) * K_PASS, cols].rearrange("(p t) n -> p t n", t=PACK)
            )
            return raw

        def load_w1_unit(q, g):
            raw = raw_pool.tile([P, PACK, UNIT], BF16, name="w1_raw%d_%d" % (q, g), tag="raw")
            nc.sync.dma_start(
                out=raw[:],
                in_=w1[g * K_PASS : (g + 1) * K_PASS, q * UNIT : (q + 1) * UNIT].rearrange(
                    "(p t) n -> p t n", t=PACK
                ),
            )
            return raw

        units = []
        nc.sync.dma_start(out=attn_sb[0][:], in_=attn_rows[0:P, :])
        for g in range(PASSES):
            for n in range(D // BANK):
                cols = slice(n * BANK, (n + 1) * BANK)
                units.append((load_wo_unit(g, cols), wo_codes[:, g, cols], wo_scales[:, g, cols]))
        nc.sync.dma_start(out=bo_row[0:1, :], in_=bo.unsqueeze(0))
        nc.sync.dma_start(out=x_sb[0][:], in_=x_rows[0:P, :])
        for q in range(QUARTERS):
            cols = slice(q * UNIT, (q + 1) * UNIT)
            for g in range(PASSES):
                units.append((load_w1_unit(q, g), w1_codes[:, g, cols], w1_scales[:, g, cols]))
                if q == 0:
                    load_tokens(g + 1)
                    if g == 0:
                        nc.sync.dma_start(out=gain_all[:], in_=mlp_norm_w.partition_broadcast(P))
            if q == 1:
                nc.sync.dma_start(out=b1_all[:], in_=b1.partition_broadcast(P))
        for j in range(LAG, TOKEN_TILES):
            load_tokens(j)

        grouped_tiles = []

        def weight_step(s):
            if s < WEIGHT_UNITS:
                raw = units[s][0]
                width = raw.shape[2]
                grouped = grouped_pool.tile([P, width, PACK], BF16, align_bytes=64)
                half = width // 2
                nc.vector.tensor_copy(
                    out=grouped[:, 0:half, :].rearrange("p (c i) t -> p c t i", i=4),
                    in_=raw[:, :, 0:half].rearrange("p t (c i) -> p c t i", i=4),
                )
                nc.scalar.copy(
                    out=grouped[:, half:width, :].rearrange("p (c i) t -> p c t i", i=4),
                    in_=raw[:, :, half:width].rearrange("p t (c i) -> p c t i", i=4),
                )
                grouped_tiles.append(grouped)
            if s >= 1:
                nc.vector.quantize_mx(
                    out=units[s - 1][1].bitcast(FP8X4),
                    scales=units[s - 1][2],
                    in_=grouped_tiles[s - 1][:].rearrange("p w t -> p (w t)"),
                )

        attn_grouped, attn_mx, x_bo, acc_1, x_mid, inv_rms, h, h_grouped, h_mx = ({} for n in range(9))

        def transpose_attn(j):
            words = attn_sb[j][:].bitcast(F32)
            attn_t = psum_t.tile([P, PACK, P], F32)
            for g in range(PASSES):
                for u in range(2):
                    nc.tensor.transpose(
                        attn_t[:, 2 * g + u, :], words[:, 2 * P * g + u : 2 * P * (g + 1) : 2], ident_f32[:]
                    )
            grouped = work.tile([P, PASSES * P * PACK], BF16, align_bytes=64, name="attn_grouped")
            nc.scalar.copy(
                out=grouped[:].bitcast(F32).rearrange("p (g r u) -> p g r u", g=PASSES, u=2),
                in_=attn_t[:].rearrange("p (g u) r -> p g r u", u=2),
            )
            attn_grouped[j] = grouped

        def quantise_attn(j):
            codes = work.tile([P, PASSES * P], U32, align_bytes=64, name="attn_codes")
            scales = work.tile([P, PASSES * P], U8, align_bytes=64, name="attn_scales")
            nc.vector.quantize_mx(out=codes[:].bitcast(FP8X4), scales=scales[:], in_=attn_grouped[j][:])
            attn_mx[j] = (codes, scales)

        def add_bo_to_x(j):
            total = work.tile([P, D], F32, name="x_bo")
            for n in range(D // BANK):
                cols = slice(n * BANK, (n + 1) * BANK)
                bank = psum_x.tile([P, BANK], F32)
                nc.tensor.matmul(out=bank[:], lhsT=ident_bf16[:], rhs=x_sb[j][:, cols], start=True, stop=False)
                nc.tensor.matmul(out=bank[:], lhsT=ones[:], rhs=bo_row[:, cols], start=False, stop=True)
                nc.scalar.copy(out=total[:, cols], in_=bank[:])
            x_bo[j] = total

        def first_matmul(j):
            codes, scales = attn_mx[j]
            acc_1[j] = []
            for n in range(D // BANK):
                cols = slice(n * BANK, (n + 1) * BANK)
                acc = psum_1.tile([P, BANK], F32, name="acc_1")
                for g in range(PASSES):
                    toks = slice(g * P, (g + 1) * P)
                    nc.tensor.matmul_mx(
                        out=acc[:],
                        lhsT=codes[:, toks].bitcast(FP8X4),
                        lhsT_scale=scales[:, toks],
                        rhs=wo_codes[:, g, cols].bitcast(FP8X4),
                        rhs_scale=wo_scales[:, g, cols],
                        start=(g == 0),
                        stop=(g == PASSES - 1),
                    )
                acc_1[j].append(acc)

        def residual_and_rms(j):
            total = work.tile([P, D], F32, name="x_mid", bufs=3)
            for n in range(D // BANK):
                cols = slice(n * BANK, (n + 1) * BANK)
                nc.vector.tensor_tensor(out=total[:, cols], in0=acc_1[j][n][:], in1=x_bo[j][:, cols], op=ALU.add)
            nc.sync.dma_start(out=x_mid_rows[j * P : (j + 1) * P, :], in_=total[:])
            squares = work.tile([P, D], BF16)
            mean_sq = work.tile([P, 1], F32)
            nc.scalar.activation(out=squares[:], in_=total[:], func=ACT.Square, scale=D**-0.5, accum_out=mean_sq[:])
            mean_eps = work.tile([P, 1], F32)
            nc.gpsimd.tensor_scalar(out=mean_eps[:], in0=mean_sq[:], scalar1=EPS, scalar2=None, op0=ALU.add)
            power = work.tile([P, 1], F32, name="inv_rms")
            nc.gpsimd.tensor_tensor(out=power[:], in0=mean_eps[:], in1=minus_half[:], op=ALU.pow)
            x_mid[j] = total
            inv_rms[j] = power

        def normalise(j):
            normed = work.tile([P, D], BF16, name="h")
            nc.vector.scalar_tensor_tensor(
                out=normed[:], in0=x_mid[j][:], scalar=inv_rms[j][:, 0:1], in1=gain_all[:], op0=ALU.mult, op1=ALU.mult
            )
            h[j] = normed

        def transpose_h(j):
            words = h[j][:].bitcast(F32)
            h_t = psum_t.tile([P, PACK, P], F32)
            for g in range(PASSES):
                for u in range(2):
                    nc.tensor.transpose(
                        h_t[:, 2 * g + u, :], words[:, 2 * P * g + u : 2 * P * (g + 1) : 2], ident_f32[:]
                    )
            grouped = work.tile([P, PASSES * P * PACK], BF16, align_bytes=64, name="h_grouped")
            nc.scalar.copy(
                out=grouped[:].bitcast(F32).rearrange("p (g r u) -> p g r u", g=PASSES, u=2),
                in_=h_t[:].rearrange("p (g u) r -> p g r u", u=2),
            )
            h_grouped[j] = grouped

        def quantise_h(j):
            codes = work.tile([P, PASSES * P], U32, align_bytes=64, name="h_codes")
            scales = work.tile([P, PASSES * P], U8, align_bytes=64, name="h_scales")
            nc.vector.quantize_mx(
                out=codes[:].bitcast(FP8X4), scales=scales[:], in_=h_grouped[j][:]
            )
            h_mx[j] = (codes, scales)

        def second_stage(j, q):
            codes, scales = h_mx[j]
            g_tile = result.tile([P, UNIT], F32)
            for n in range(UNIT // BANK):
                cols = slice(q * UNIT + n * BANK, q * UNIT + (n + 1) * BANK)
                acc = psum_2.tile([P, BANK], F32, name="acc_2")
                for g in range(PASSES):
                    toks = slice(g * P, (g + 1) * P)
                    nc.tensor.matmul_mx(
                        out=acc[:],
                        lhsT=codes[:, toks].bitcast(FP8X4),
                        lhsT_scale=scales[:, toks],
                        rhs=w1_codes[:, g, cols].bitcast(FP8X4),
                        rhs_scale=w1_scales[:, g, cols],
                        start=(g == 0),
                        stop=(g == PASSES - 1),
                    )
                nc.vector.tensor_tensor(
                    out=g_tile[:, n * BANK : (n + 1) * BANK], in0=acc[:], in1=b1_all[:, cols], op=ALU.add
                )
            nc.scalar.activation(out=g_tile[:], in_=g_tile[:], func=ACT.Gelu)
            nc.sync.dma_start(out=g_rows[j * P : (j + 1) * P, q * UNIT : (q + 1) * UNIT], in_=g_tile[:])

        def live(j):
            return 0 <= j < TOKEN_TILES

        steps_a_round = (WEIGHT_UNITS + 1 + LAG - 1) // LAG
        for i in range(-LAG, TOKEN_TILES):
            if live(i + 3):
                transpose_attn(i + 3)
            if live(i + 1):
                transpose_h(i + 1)
            if live(i + 2):
                residual_and_rms(i + 2)
            if live(i + 3):
                add_bo_to_x(i + 3)
                quantise_attn(i + 3)
            if live(i + 1):
                quantise_h(i + 1)
            if i < 0:
                first_step = (i + LAG) * steps_a_round
                for s in range(first_step, min(first_step + steps_a_round, WEIGHT_UNITS + 1)):
                    weight_step(s)
            else:
                for q in range(QUARTERS - 1):
                    second_stage(i, q)
            if live(i + 2):
                normalise(i + 2)
            if i >= 0:
                second_stage(i, QUARTERS - 1)
            if live(i + 3):
                first_matmul(i + 3)
